import numpy as np
import ml_dtypes


def mxq(x, axis, fmt="e4m3"):
    dtype, down = {"e4m3": (ml_dtypes.float8_e4m3fn, 7), "e5m2": (ml_dtypes.float8_e5m2, 14)}[fmt]
    v = np.moveaxis(np.asarray(x, np.float32).astype(ml_dtypes.bfloat16).astype(np.float64), axis, -1)
    blocks = v.reshape(v.shape[:-1] + (-1, 32))
    amax = np.abs(blocks).max(-1, keepdims=True)
    byte = np.maximum(np.where(amax > 0, np.frexp(amax)[1] - 1 + 127, 0) - down, 1)
    scale = np.exp2(byte - 127.0)
    codes = (blocks / scale).astype(np.float32).astype(dtype).astype(np.float64)
    return np.moveaxis((codes * scale).reshape(v.shape), -1, axis)


WIDE = False


def mx_kscale(k):
    if not WIDE:
        return np.ones(k)
    levels = np.array([10, -10, 5, -5, 0])
    if k % 512:
        return np.exp2(np.random.permutation(np.resize(levels, k // 32))).repeat(32)
    a = np.empty((k // 512, 16))
    for p in range(k // 512):
        a[p, :8] = np.random.permutation(np.resize(levels, 8))
        for g in range(8):
            far = levels[np.abs(levels - a[p, g]) >= 10]
            a[p, g + 8] = far[np.random.randint(len(far))]
    return np.exp2(a.ravel()).repeat(32)


BF16 = ml_dtypes.bfloat16


def bf(x):
    return np.asarray(x, np.float32).astype(BF16)


def f64(x):
    return np.asarray(x).astype(np.float64)


SL, BS, DM, H, NH, DO = 64, 128, 1024, 4, 64, 1024
DP = H * NH


def log_softmax0(x):
    z = x - x.max(0, keepdims=True)
    return z - np.log(np.exp(z).sum(0, keepdims=True))


def setup_inputs():
    s, u = mx_kscale(DM), mx_kscale(DM)
    return {"query": bf(np.random.standard_normal((BS, DM)) * 2.0 * s),
            "keys": bf(np.random.standard_normal((SL, BS, DM)) * u),
            "Wq": bf(np.random.standard_normal((DP, DM)) / np.sqrt(DM) / s),
            "Wk": bf(np.random.standard_normal((DP, DM)) / np.sqrt(DM) / u)}


def reference(query, keys, Wq, Wk):
    qp = mxq(f64(query), 1, "e4m3") @ mxq(f64(Wq), 1, "e4m3").T
    kp = mxq(f64(keys), 2, "e4m3") @ mxq(f64(Wk), 1, "e4m3").T
    dot = (qp * kp).reshape(SL, BS, H, NH).sum(-1) / np.sqrt(NH)
    return log_softmax0(dot)

@@ -1,0 +1,273 @@
+import math
+from contextlib import ExitStack
+
+import concourse.mybir as mybir
+from concourse.masks import make_identity
+
+F32 = mybir.dt.float32
+BF16 = mybir.dt.bfloat16
+U32 = mybir.dt.uint32
+U8 = mybir.dt.uint8
+FP8X4 = mybir.dt.float8_e4m3fn_x4
+ALU = mybir.AluOpType
+ACT = mybir.ActivationFunctionType
+AXIS = mybir.AxisListType
+
+SL, BS, DM, H, NH = 64, 128, 1024, 4, 64
+DP = H * NH
+P = 128
+PACK = 4
+K_PASS = P * PACK
+PASSES = DM // K_PASS
+WORDS = DM // 2
+CHUNKS = WORDS // P
+HALVES = CHUNKS // PASSES
+S_LOAD = 2
+S_ROUND = 2
+ROUNDS = SL // S_ROUND
+S_BANK = 512 // DP
+H_VECTOR = 3
+LAG_PROJECT = 2
+LAG_MULTIPLY = 4
+LAG_SUM = 5
+
+FLOPS = 2 * (SL + 1) * BS * DM * DP
+
+
+def transpose_rows(nc, banks, ident, row_words):
+    bank = banks.tile([P, CHUNKS, P], F32)
+    for c in range(CHUNKS):
+        g, u = divmod(c, HALVES)
+        first = g * HALVES * P + u
+        nc.tensor.transpose(
+            bank[:, c, :], row_words[:, first : (g + 1) * HALVES * P : HALVES], ident[:]
+        )
+    return bank
+
+
+def by_pass_row_half(bank):
+    return bank[:].rearrange("p (g u) r -> p g r u", u=HALVES)
+
+
+def tile_multiheadattention_pa_t_kernel(tc, query, keys, Wq, Wk, out):
+    nc = tc.nc
+    with ExitStack() as ctx:
+        const = ctx.enter_context(tc.tile_pool(name="const", bufs=1))
+        resident = ctx.enter_context(tc.tile_pool(name="resident", bufs=SL // S_LOAD))
+        stage = ctx.enter_context(tc.tile_pool(name="stage", bufs=4))
+        banks = ctx.enter_context(tc.psum_pool(name="banks", bufs=4))
+        sums = ctx.enter_context(tc.psum_pool(name="sums", bufs=4))
+        ctx.enter_context(tc.manual_schedule())
+
+        key_rows = []
+
+        def load_keys(first, last):
+            for i in range(first, last):
+                rows = resident.tile([P, S_LOAD * DM], BF16, name="rows")
+                nc.sync.dma_start(
+                    out=rows[:].rearrange("b (s k) -> b s k", s=S_LOAD),
+                    in_=keys[i * S_LOAD : (i + 1) * S_LOAD].rearrange("s b k -> b s k"),
+                )
+                key_rows.append(rows)
+
+        wk_rows = const.tile([P, (DP // P) * DM], BF16)
+        wq_rows = const.tile([P, (DP // P) * DM], BF16)
+        q_rows = const.tile([P, DM], BF16)
+        nc.sync.dma_start(out=q_rows[:], in_=query)
+        nc.sync.dma_start(
+            out=wq_rows[:].rearrange("p (r k) -> p r k", k=DM),
+            in_=Wq.rearrange("(r p) k -> p r k", p=P),
+        )
+        nc.sync.dma_start(
+            out=wk_rows[:].rearrange("p (r k) -> p r k", k=DM),
+            in_=Wk.rearrange("(r p) k -> p r k", p=P),
+        )
+        load_keys(0, SL // S_LOAD)
+
+        ident = const.tile([P, P], F32)
+        make_identity(nc, ident[:])
+        dot = const.tile([P, H, SL], F32)
+        result = const.tile([P, (H + 1) * SL], F32)
+        nc.gpsimd.memset(result[:, H * SL :], 0.0)
+
+        def quantise_weight(w_rows, name):
+            grouped = const.tile([P, PASSES * DP * PACK], BF16, align_bytes=64, name=name + "_grouped")
+            words = grouped[:].bitcast(F32).rearrange(
+                "p (g r c u) -> p g r c u", g=PASSES, r=DP // P, u=HALVES
+            )
+            for r in range(DP // P):
+                bank = transpose_rows(nc, banks, ident, w_rows[:].bitcast(F32)[:, r * WORDS : (r + 1) * WORDS])
+                nc.scalar.copy(out=words[:, :, r, :, :], in_=by_pass_row_half(bank))
+            codes = const.tile([P, PASSES * DP], U32, align_bytes=64, name=name + "_codes")
+            scales = const.tile([P, PASSES * DP], U8, align_bytes=64, name=name + "_scales")
+            nc.vector.quantize_mx(out=codes[:].bitcast(FP8X4), scales=scales[:], in_=grouped[:])
+            return codes, scales
+
+        def project(acc, row_codes, row_scales, first_col, w_codes, w_scales):
+            for g in range(PASSES):
+                rows = slice(first_col + g * P, first_col + (g + 1) * P)
+                chans = slice(g * DP, (g + 1) * DP)
+                nc.tensor.matmul_mx(
+                    out=acc,
+                    lhsT=row_codes[:, rows].bitcast(FP8X4),
+                    lhsT_scale=row_scales[:, rows],
+                    rhs=w_codes[:, chans].bitcast(FP8X4),
+                    rhs_scale=w_scales[:, chans],
+                    start=(g == 0),
+                    stop=(g == PASSES - 1),
+                )
+
+        def quantise_query():
+            grouped = const.tile([P, DM], BF16, align_bytes=64, name="q_grouped")
+            bank = transpose_rows(nc, banks, ident, q_rows[:].bitcast(F32))
+            nc.scalar.copy(
+                out=grouped[:].bitcast(F32).rearrange("p (g r u) -> p g r u", g=PASSES, u=HALVES),
+                in_=by_pass_row_half(bank),
+            )
+            codes = const.tile([P, PASSES * P], U32, align_bytes=64, name="q_codes")
+            scales = const.tile([P, PASSES * P], U8, align_bytes=64, name="q_scales")
+            nc.vector.quantize_mx(out=codes[:].bitcast(FP8X4), scales=scales[:], in_=grouped[:])
+            return codes, scales
+
+        def project_query(q_codes, q_scales, wq_codes, wq_scales):
+            acc = sums.tile([P, S_BANK * DP], F32, name="acc")
+            project(acc[:, :DP], q_codes, q_scales, 0, wq_codes, wq_scales)
+            qp = const.tile([P, DP], F32)
+            nc.scalar.mul(out=qp[:], in_=acc[:, :DP], mul=1.0 / math.sqrt(NH))
+            return qp
+
+        grouped_of = {}
+        codes_of = {}
+        acc_of = {}
+        prod_of = {}
+        folded_of = {}
+
+        def transpose_round(i):
+            grouped = stage.tile([P, S_ROUND * DM], BF16, align_bytes=64, name="grouped")
+            words = grouped[:].bitcast(F32)
+            for j in range(S_ROUND):
+                s = i * S_ROUND + j
+                rows = key_rows[s // S_LOAD][:].bitcast(F32)
+                first = (s % S_LOAD) * WORDS
+                bank = transpose_rows(nc, banks, ident, rows[:, first : first + WORDS])
+                nc.scalar.copy(
+                    out=words[:, j * WORDS : (j + 1) * WORDS].rearrange(
+                        "p (g r u) -> p g r u", g=PASSES, u=HALVES
+                    ),
+                    in_=by_pass_row_half(bank),
+                )
+            grouped_of[i] = grouped
+
+        def quantise_round(i):
+            codes = stage.tile([P, S_ROUND * PASSES * P], U32, align_bytes=64, name="codes")
+            scales = stage.tile([P, S_ROUND * PASSES * P], U8, align_bytes=64, name="scales")
+            nc.vector.quantize_mx(out=codes[:].bitcast(FP8X4), scales=scales[:], in_=grouped_of[i][:])
+            codes_of[i] = (codes, scales)
+
+        def project_round(i, wk_codes, wk_scales):
+            codes, scales = codes_of[i]
+            acc_of[i] = []
+            for half in range(S_ROUND // S_BANK):
+                acc = sums.tile([P, S_BANK * DP], F32, name="acc")
+                for j in range(S_BANK):
+                    first_col = (half * S_BANK + j) * PASSES * P
+                    project(acc[:, j * DP : (j + 1) * DP], codes, scales, first_col, wk_codes, wk_scales)
+                acc_of[i].append(acc)
+
+        def multiply_round(i, qp):
+            prod = stage.tile([P, S_ROUND * DP], F32, name="prod")
+            for half, acc in enumerate(acc_of[i]):
+                nc.vector.tensor_tensor(
+                    out=prod[:, half * S_BANK * DP : (half + 1) * S_BANK * DP].rearrange(
+                        "p (s c) -> p s c", s=S_BANK
+                    ),
+                    in0=acc[:].rearrange("p (s c) -> p s c", s=S_BANK),
+                    in1=qp[:].unsqueeze(1).to_broadcast([P, S_BANK, DP]),
+                    op=ALU.mult,
+                )
+            prod_of[i] = prod
+
+        def fold_round(i):
+            halves = prod_of[i][:].rearrange("p (s h t j) -> p s h t j", s=S_ROUND, h=H, t=2)
+            folded = stage.tile([P, S_ROUND, H_VECTOR, NH // 2], F32, name="folded")
+            nc.gpsimd.tensor_tensor(
+                out=folded[:],
+                in0=halves[:, :, :H_VECTOR, 0, :],
+                in1=halves[:, :, :H_VECTOR, 1, :],
+                op=ALU.add,
+            )
+            folded_of[i] = folded
+            by_head = prod_of[i][:].rearrange("p (s h j) -> p s h j", s=S_ROUND, h=H)
+            unused = stage.tile([P, S_ROUND, H - H_VECTOR, NH], F32, name="unused")
+            for j in range(S_ROUND):
+                s = i * S_ROUND + j
+                for h in range(H_VECTOR, H):
+                    nc.scalar.activation(
+                        out=unused[:, j, h - H_VECTOR, :],
+                        in_=by_head[:, j, h, :],
+                        func=ACT.Copy,
+                        accum_out=dot[:, h, s : s + 1],
+                    )
+
+        def sum_round(i):
+            nc.vector.tensor_reduce(
+                out=dot[:, :H_VECTOR, i * S_ROUND : (i + 1) * S_ROUND],
+                in_=folded_of[i][:].rearrange("p s h j -> p h s j"),
+                axis=AXIS.X,
+                op=ALU.add,
+            )
+
+        def live(i):
+            return 0 <= i < ROUNDS
+
+        q_codes, q_scales = quantise_query()
+        wq_codes, wq_scales = quantise_weight(wq_rows, "wq")
+        wk_codes, wk_scales = quantise_weight(wk_rows, "wk")
+        transpose_round(0)
+        qp = project_query(q_codes, q_scales, wq_codes, wq_scales)
+        for step in range(1, ROUNDS + LAG_SUM):
+            if live(step):
+                transpose_round(step)
+            if live(step - LAG_MULTIPLY):
+                multiply_round(step - LAG_MULTIPLY, qp)
+            if live(step - LAG_PROJECT):
+                quantise_round(step - LAG_PROJECT)
+                project_round(step - LAG_PROJECT, wk_codes, wk_scales)
+            if live(step - LAG_MULTIPLY):
+                fold_round(step - LAG_MULTIPLY)
+            if live(step - LAG_SUM):
+                sum_round(step - LAG_SUM)
+
+        neg_max = const.tile([P, H], F32)
+        nc.vector.tensor_reduce(out=neg_max[:], in_=dot[:], axis=AXIS.X, op=ALU.max, negate=True)
+        expd = const.tile([P, H, SL], F32)
+        exp_sum = const.tile([P, H], F32)
+        for h in range(H):
+            nc.scalar.activation(
+                out=expd[:, h, :],
+                in_=dot[:, h, :],
+                func=ACT.Exp,
+                bias=neg_max[:, h : h + 1],
+                scale=1.0,
+                accum_out=exp_sum[:, h : h + 1],
+            )
+        log_sum = const.tile([P, H], F32)
+        nc.scalar.activation(out=log_sum[:], in_=exp_sum[:], func=ACT.Ln)
+        shift = const.tile([P, H], F32)
+        nc.vector.tensor_tensor(out=shift[:], in0=log_sum[:], in1=neg_max[:], op=ALU.subtract)
+        nc.vector.tensor_tensor(
+            out=result[:, : H * SL].rearrange("p (h s) -> p h s", h=H),
+            in0=dot[:],
+            in1=shift[:].unsqueeze(2).to_broadcast([P, H, SL]),
+            op=ALU.subtract,
+        )
+
+        flipped = banks.tile([P, H, P], F32, name="bank")
+        for h in range(H):
+            nc.tensor.transpose(flipped[:, h, :], result[:, h * SL : h * SL + P], ident[:])
+        rows_out = const.tile([P, BS, H], F32)
+        nc.vector.tensor_copy(out=rows_out[:], in_=flipped[:].rearrange("p h b -> p b h"))
+        nc.sync.dma_start(
+            out=out.rearrange("s b h -> s (b h)"),
+            in_=rows_out[:SL].rearrange("s b h -> s (b h)"),
+        )

@@ -87,8 +87,8 @@ def tile_multiheadattention_pa_t_kernel(tc, query, keys, Wq, Wk, out):
         ident = const.tile([P, P], F32)
         make_identity(nc, ident[:])
         dot = const.tile([P, H, SL], F32)
-        result = const.tile([P, (H + 1) * SL], F32)
-        nc.gpsimd.memset(result[:, H * SL :], 0.0)
+        shifted = const.tile([P, (H + 1) * SL], F32)
+        nc.gpsimd.memset(shifted[:, H * SL :], 0.0)
 
         def quantise_weight(w_rows, name):
             grouped = const.tile([P, PASSES * DP * PACK], BF16, align_bytes=64, name=name + "_grouped")
@@ -251,23 +251,33 @@ def tile_multiheadattention_pa_t_kernel(tc, query, keys, Wq, Wk, out):
                 scale=1.0,
                 accum_out=exp_sum[:, h : h + 1],
             )
-        log_sum = const.tile([P, H], F32)
-        nc.scalar.activation(out=log_sum[:], in_=exp_sum[:], func=ACT.Ln)
-        shift = const.tile([P, H], F32)
-        nc.vector.tensor_tensor(out=shift[:], in0=log_sum[:], in1=neg_max[:], op=ALU.subtract)
         nc.vector.tensor_tensor(
-            out=result[:, : H * SL].rearrange("p (h s) -> p h s", h=H),
+            out=shifted[:, : H * SL].rearrange("p (h s) -> p h s", h=H),
             in0=dot[:],
-            in1=shift[:].unsqueeze(2).to_broadcast([P, H, SL]),
-            op=ALU.subtract,
+            in1=neg_max[:].unsqueeze(2).to_broadcast([P, H, SL]),
+            op=ALU.add,
         )
 
         flipped = banks.tile([P, H, P], F32, name="bank")
         for h in range(H):
-            nc.tensor.transpose(flipped[:, h, :], result[:, h * SL : h * SL + P], ident[:])
-        rows_out = const.tile([P, BS, H], F32)
-        nc.vector.tensor_copy(out=rows_out[:], in_=flipped[:].rearrange("p h b -> p b h"))
-        nc.sync.dma_start(
-            out=out.rearrange("s b h -> s (b h)"),
-            in_=rows_out[:SL].rearrange("s b h -> s (b h)"),
-        )
+            nc.tensor.transpose(flipped[:, h, :], shifted[:, h * SL : h * SL + P], ident[:])
+        spread = banks.tile([P, H, P], F32, name="bank")
+        for h in range(H):
+            nc.tensor.transpose(spread[:, h, :], exp_sum[:, h : h + 1].to_broadcast([P, P]), ident[:])
+        for first in range(0, BS, BS // 2):
+            half = slice(first, first + BS // 2)
+            log_sum = const.tile([P, BS // 2, H], F32, name=f"log_sum_{first}")
+            nc.scalar.activation(
+                out=log_sum[:SL], in_=spread[:SL, :, half].rearrange("s h b -> s b h"), func=ACT.Ln
+            )
+            rows_out = const.tile([P, BS // 2, H], F32, name=f"rows_out_{first}")
+            nc.vector.tensor_tensor(
+                out=rows_out[:SL],
+                in0=flipped[:SL, :, half].rearrange("s h b -> s b h"),
+                in1=log_sum[:SL],
+                op=ALU.subtract,
+            )
+            nc.sync.dma_start(
+                out=out[:, half, :].rearrange("s b h -> s (b h)"),
+                in_=rows_out[:SL].rearrange("s b h -> s (b h)"),
+            )

@@ -23,30 +23,49 @@ WORDS = DM // 2
 CHUNKS = WORDS // P
 HALVES = CHUNKS // PASSES
 S_LOAD = 2
-S_ROUND = 2
-ROUNDS = SL // S_ROUND
 S_BANK = 512 // DP
-H_VECTOR = 3
+ROUND_STEPS = (2,) * 31 + (1, 1)
+ROUNDS = len(ROUND_STEPS)
+MAX_STEPS = max(ROUND_STEPS)
 LAG_PROJECT = 2
 LAG_MULTIPLY = 4
 LAG_SUM = 5
+H_FOLD = 2
+H_VECTOR = 3
+RUN = 8
 
 FLOPS = 2 * (SL + 1) * BS * DM * DP
 
 
-def transpose_rows(nc, banks, ident, row_words):
+def every_second(row_words, g, u):
+    first = g * HALVES * P + u
+    return row_words[:, first : (g + 1) * HALVES * P : HALVES]
+
+
+def from_split(split_words, g, u):
+    first = (u * PASSES + g) * P
+    return split_words[:, first : first + P]
+
+
+def transpose_rows(nc, banks, ident, row_words, pick):
     bank = banks.tile([P, CHUNKS, P], F32)
     for c in range(CHUNKS):
         g, u = divmod(c, HALVES)
-        first = g * HALVES * P + u
-        nc.tensor.transpose(
-            bank[:, c, :], row_words[:, first : (g + 1) * HALVES * P : HALVES], ident[:]
-        )
+        nc.tensor.transpose(bank[:, c, :], pick(row_words, g, u), ident[:])
     return bank
 
 
 def by_pass_row_half(bank):
     return bank[:].rearrange("p (g u) r -> p g r u", u=HALVES)
+
+
+def split_rows(nc, pool, rows, name):
+    split = pool.tile([P, DM], BF16, name=name)
+    nc.vector.tensor_copy(
+        out=split[:].rearrange("p (u c e) -> p u c e", u=HALVES, e=2 * RUN),
+        in_=rows.rearrange("p (c u e) -> p u c e", u=HALVES, e=2 * RUN),
+    )
+    return split
 
 
 def tile_multiheadattention_pa_t_kernel(tc, query, keys, Wq, Wk, out):
@@ -70,19 +89,20 @@ def tile_multiheadattention_pa_t_kernel(tc, query, keys, Wq, Wk, out):
                 )
                 key_rows.append(rows)
 
-        wk_rows = const.tile([P, (DP // P) * DM], BF16)
-        wq_rows = const.tile([P, (DP // P) * DM], BF16)
+        def load_weight(w, name):
+            parts = []
+            for r in range(DP // P):
+                part = const.tile([P, DM], BF16, name=f"{name}_rows_{r}")
+                nc.sync.dma_start(out=part[:], in_=w[r * P : (r + 1) * P])
+                parts.append(part)
+            return parts
+
+        wk_rows = load_weight(Wk, "wk")
+        load_keys(0, 1)
         q_rows = const.tile([P, DM], BF16)
         nc.sync.dma_start(out=q_rows[:], in_=query)
-        nc.sync.dma_start(
-            out=wq_rows[:].rearrange("p (r k) -> p r k", k=DM),
-            in_=Wq.rearrange("(r p) k -> p r k", p=P),
-        )
-        nc.sync.dma_start(
-            out=wk_rows[:].rearrange("p (r k) -> p r k", k=DM),
-            in_=Wk.rearrange("(r p) k -> p r k", p=P),
-        )
-        load_keys(0, SL // S_LOAD)
+        wq_rows = load_weight(Wq, "wq")
+        load_keys(1, SL // S_LOAD)
 
         ident = const.tile([P, P], F32)
         make_identity(nc, ident[:])
@@ -90,16 +110,22 @@ def tile_multiheadattention_pa_t_kernel(tc, query, keys, Wq, Wk, out):
         shifted = const.tile([P, (H + 1) * SL], F32)
         nc.gpsimd.memset(shifted[:, H * SL :], 0.0)
 
-        def quantise_weight(w_rows, name):
+        def group_weight(parts, pick, name):
             grouped = const.tile([P, PASSES * DP * PACK], BF16, align_bytes=64, name=name + "_grouped")
             words = grouped[:].bitcast(F32).rearrange(
                 "p (g r c u) -> p g r c u", g=PASSES, r=DP // P, u=HALVES
             )
-            for r in range(DP // P):
-                bank = transpose_rows(nc, banks, ident, w_rows[:].bitcast(F32)[:, r * WORDS : (r + 1) * WORDS])
-                nc.scalar.copy(out=words[:, :, r, :, :], in_=by_pass_row_half(bank))
-            codes = const.tile([P, PASSES * DP], U32, align_bytes=64, name=name + "_codes")
-            scales = const.tile([P, PASSES * DP], U8, align_bytes=64, name=name + "_scales")
+            for part, r, copy in zip(parts, range(DP // P), (nc.scalar.copy, nc.vector.tensor_copy)):
+                bank = transpose_rows(nc, banks, ident, part[:].bitcast(F32), pick)
+                copy(out=words[:, :, r, :, :], in_=by_pass_row_half(bank))
+            return grouped
+
+        def split_weight(parts, name):
+            return [split_rows(nc, const, part[:], f"{name}_split_{r}") for r, part in enumerate(parts)]
+
+        def quantise(grouped, columns, name):
+            codes = const.tile([P, columns], U32, align_bytes=64, name=name + "_codes")
+            scales = const.tile([P, columns], U8, align_bytes=64, name=name + "_scales")
             nc.vector.quantize_mx(out=codes[:].bitcast(FP8X4), scales=scales[:], in_=grouped[:])
             return codes, scales
 
@@ -117,21 +143,18 @@ def tile_multiheadattention_pa_t_kernel(tc, query, keys, Wq, Wk, out):
                     stop=(g == PASSES - 1),
                 )
 
-        def quantise_query():
+        def group_query(q_split):
             grouped = const.tile([P, DM], BF16, align_bytes=64, name="q_grouped")
-            bank = transpose_rows(nc, banks, ident, q_rows[:].bitcast(F32))
+            bank = transpose_rows(nc, banks, ident, q_split[:].bitcast(F32), from_split)
             nc.scalar.copy(
                 out=grouped[:].bitcast(F32).rearrange("p (g r u) -> p g r u", g=PASSES, u=HALVES),
                 in_=by_pass_row_half(bank),
             )
-            codes = const.tile([P, PASSES * P], U32, align_bytes=64, name="q_codes")
-            scales = const.tile([P, PASSES * P], U8, align_bytes=64, name="q_scales")
-            nc.vector.quantize_mx(out=codes[:].bitcast(FP8X4), scales=scales[:], in_=grouped[:])
-            return codes, scales
+            return grouped
 
-        def project_query(q_codes, q_scales, wq_codes, wq_scales):
+        def project_query(q_mx, wq_mx):
             acc = sums.tile([P, S_BANK * DP], F32, name="acc")
-            project(acc[:, :DP], q_codes, q_scales, 0, wq_codes, wq_scales)
+            project(acc[:, :DP], *q_mx, 0, *wq_mx)
             qp = const.tile([P, DP], F32)
             nc.scalar.mul(out=qp[:], in_=acc[:, :DP], mul=1.0 / math.sqrt(NH))
             return qp
@@ -142,14 +165,25 @@ def tile_multiheadattention_pa_t_kernel(tc, query, keys, Wq, Wk, out):
         prod_of = {}
         folded_of = {}
 
+        def live(i):
+            return 0 <= i < ROUNDS
+
+        def first_step(i):
+            return sum(ROUND_STEPS[:i])
+
+        def full(i):
+            return ROUND_STEPS[i] == MAX_STEPS
+
+        def step_rows(s):
+            first = (s % S_LOAD) * DM
+            return key_rows[s // S_LOAD][:, first : first + DM]
+
         def transpose_round(i):
-            grouped = stage.tile([P, S_ROUND * DM], BF16, align_bytes=64, name="grouped")
+            grouped = stage.tile([P, MAX_STEPS * DM], BF16, align_bytes=64, name="grouped")
             words = grouped[:].bitcast(F32)
-            for j in range(S_ROUND):
-                s = i * S_ROUND + j
-                rows = key_rows[s // S_LOAD][:].bitcast(F32)
-                first = (s % S_LOAD) * WORDS
-                bank = transpose_rows(nc, banks, ident, rows[:, first : first + WORDS])
+            for j in range(ROUND_STEPS[i]):
+                s = first_step(i) + j
+                bank = transpose_rows(nc, banks, ident, step_rows(s).bitcast(F32), every_second)
                 nc.scalar.copy(
                     out=words[:, j * WORDS : (j + 1) * WORDS].rearrange(
                         "p (g r u) -> p g r u", g=PASSES, u=HALVES
@@ -159,80 +193,97 @@ def tile_multiheadattention_pa_t_kernel(tc, query, keys, Wq, Wk, out):
             grouped_of[i] = grouped
 
         def quantise_round(i):
-            codes = stage.tile([P, S_ROUND * PASSES * P], U32, align_bytes=64, name="codes")
-            scales = stage.tile([P, S_ROUND * PASSES * P], U8, align_bytes=64, name="scales")
-            nc.vector.quantize_mx(out=codes[:].bitcast(FP8X4), scales=scales[:], in_=grouped_of[i][:])
+            columns = ROUND_STEPS[i] * PASSES * P
+            codes = stage.tile([P, MAX_STEPS * PASSES * P], U32, align_bytes=64, name="codes")
+            scales = stage.tile([P, MAX_STEPS * PASSES * P], U8, align_bytes=64, name="scales")
+            nc.vector.quantize_mx(
+                out=codes[:, :columns].bitcast(FP8X4),
+                scales=scales[:, :columns],
+                in_=grouped_of[i][:, : columns * PACK],
+            )
             codes_of[i] = (codes, scales)
 
-        def project_round(i, wk_codes, wk_scales):
+        def project_round(i):
             codes, scales = codes_of[i]
-            acc_of[i] = []
-            for half in range(S_ROUND // S_BANK):
-                acc = sums.tile([P, S_BANK * DP], F32, name="acc")
-                for j in range(S_BANK):
-                    first_col = (half * S_BANK + j) * PASSES * P
-                    project(acc[:, j * DP : (j + 1) * DP], codes, scales, first_col, wk_codes, wk_scales)
-                acc_of[i].append(acc)
+            acc = sums.tile([P, S_BANK * DP], F32, name="acc")
+            for j in range(ROUND_STEPS[i]):
+                project(acc[:, j * DP : (j + 1) * DP], codes, scales, j * PASSES * P, *wk_mx)
+            acc_of[i] = acc
 
-        def multiply_round(i, qp):
-            prod = stage.tile([P, S_ROUND * DP], F32, name="prod")
-            for half, acc in enumerate(acc_of[i]):
-                nc.vector.tensor_tensor(
-                    out=prod[:, half * S_BANK * DP : (half + 1) * S_BANK * DP].rearrange(
-                        "p (s c) -> p s c", s=S_BANK
-                    ),
-                    in0=acc[:].rearrange("p (s c) -> p s c", s=S_BANK),
-                    in1=qp[:].unsqueeze(1).to_broadcast([P, S_BANK, DP]),
-                    op=ALU.mult,
-                )
+        def multiply_round(i):
+            steps = ROUND_STEPS[i]
+            prod = stage.tile([P, MAX_STEPS * DP], F32, name="prod")
+            nc.vector.tensor_tensor(
+                out=prod[:, : steps * DP].rearrange("p (s c) -> p s c", s=steps),
+                in0=acc_of[i][:, : steps * DP].rearrange("p (s c) -> p s c", s=steps),
+                in1=qp[:].unsqueeze(1).to_broadcast([P, steps, DP]),
+                op=ALU.mult,
+            )
             prod_of[i] = prod
 
+        def by_head(i):
+            return prod_of[i][:].rearrange("p (s h j) -> p s h j", s=MAX_STEPS, h=H)
+
         def fold_round(i):
-            halves = prod_of[i][:].rearrange("p (s h t j) -> p s h t j", s=S_ROUND, h=H, t=2)
-            folded = stage.tile([P, S_ROUND, H_VECTOR, NH // 2], F32, name="folded")
-            nc.gpsimd.tensor_tensor(
-                out=folded[:],
-                in0=halves[:, :, :H_VECTOR, 0, :],
-                in1=halves[:, :, :H_VECTOR, 1, :],
-                op=ALU.add,
-            )
-            folded_of[i] = folded
-            by_head = prod_of[i][:].rearrange("p (s h j) -> p s h j", s=S_ROUND, h=H)
-            unused = stage.tile([P, S_ROUND, H - H_VECTOR, NH], F32, name="unused")
-            for j in range(S_ROUND):
-                s = i * S_ROUND + j
+            if full(i):
+                halves = prod_of[i][:].rearrange("p (s h t j) -> p s h t j", s=MAX_STEPS, h=H, t=2)
+                folded = stage.tile([P, MAX_STEPS, H_FOLD, NH // 2], F32, name="folded")
+                nc.gpsimd.tensor_tensor(
+                    out=folded[:],
+                    in0=halves[:, :, :H_FOLD, 0, :],
+                    in1=halves[:, :, :H_FOLD, 1, :],
+                    op=ALU.add,
+                )
+                folded_of[i] = folded
+            unused = stage.tile([P, MAX_STEPS, H - H_VECTOR, NH], F32, name="unused")
+            for j in range(ROUND_STEPS[i]):
+                s = first_step(i) + j
                 for h in range(H_VECTOR, H):
                     nc.scalar.activation(
                         out=unused[:, j, h - H_VECTOR, :],
-                        in_=by_head[:, j, h, :],
+                        in_=by_head(i)[:, j, h, :],
                         func=ACT.Copy,
                         accum_out=dot[:, h, s : s + 1],
                     )
 
-        def sum_round(i):
+        def add_up(i, heads, terms):
             nc.vector.tensor_reduce(
-                out=dot[:, :H_VECTOR, i * S_ROUND : (i + 1) * S_ROUND],
-                in_=folded_of[i][:].rearrange("p s h j -> p h s j"),
+                out=dot[:, heads, first_step(i) : first_step(i) + ROUND_STEPS[i]],
+                in_=terms.rearrange("p s h j -> p h s j"),
                 axis=AXIS.X,
                 op=ALU.add,
             )
 
-        def live(i):
-            return 0 <= i < ROUNDS
+        def sum_round(i):
+            first_whole = H_FOLD if full(i) else 0
+            if first_whole < H_VECTOR:
+                add_up(
+                    i,
+                    slice(first_whole, H_VECTOR),
+                    by_head(i)[:, : ROUND_STEPS[i], first_whole:H_VECTOR, :],
+                )
+            if full(i):
+                add_up(i, slice(0, H_FOLD), folded_of[i][:])
 
-        q_codes, q_scales = quantise_query()
-        wq_codes, wq_scales = quantise_weight(wq_rows, "wq")
-        wk_codes, wk_scales = quantise_weight(wk_rows, "wk")
+        wk_grouped = group_weight(wk_rows, every_second, "wk")
         transpose_round(0)
-        qp = project_query(q_codes, q_scales, wq_codes, wq_scales)
+        q_split = split_rows(nc, const, q_rows[:], "q_split")
+        wq_split = split_weight(wq_rows, "wq")
+        wk_mx = quantise(wk_grouped, PASSES * DP, "wk")
+        q_grouped = group_query(q_split)
+        wq_grouped = group_weight(wq_split, from_split, "wq")
         for step in range(1, ROUNDS + LAG_SUM):
             if live(step):
                 transpose_round(step)
             if live(step - LAG_MULTIPLY):
-                multiply_round(step - LAG_MULTIPLY, qp)
+                multiply_round(step - LAG_MULTIPLY)
             if live(step - LAG_PROJECT):
                 quantise_round(step - LAG_PROJECT)
-                project_round(step - LAG_PROJECT, wk_codes, wk_scales)
+                project_round(step - LAG_PROJECT)
+            if step == LAG_PROJECT:
+                q_mx = quantise(q_grouped, PASSES * P, "q")
+                wq_mx = quantise(wq_grouped, PASSES * DP, "wq")
+                qp = project_query(q_mx, wq_mx)
             if live(step - LAG_MULTIPLY):
                 fold_round(step - LAG_MULTIPLY)
             if live(step - LAG_SUM):

import math
from contextlib import ExitStack

import concourse.mybir as mybir
from concourse.masks import make_identity

F32 = mybir.dt.float32
BF16 = mybir.dt.bfloat16
U32 = mybir.dt.uint32
U8 = mybir.dt.uint8
FP8X4 = mybir.dt.float8_e4m3fn_x4
ALU = mybir.AluOpType
ACT = mybir.ActivationFunctionType
AXIS = mybir.AxisListType

SL, BS, DM, H, NH = 64, 128, 1024, 4, 64
DP = H * NH
P = 128
PACK = 4
K_PASS = P * PACK
PASSES = DM // K_PASS
WORDS = DM // 2
CHUNKS = WORDS // P
HALVES = CHUNKS // PASSES
S_LOAD = 2
S_BANK = 512 // DP
ROUND_STEPS = (2,) * 31 + (1, 1)
ROUNDS = len(ROUND_STEPS)
MAX_STEPS = max(ROUND_STEPS)
LAG_PROJECT = 2
LAG_MULTIPLY = 4
LAG_SUM = 5
H_FOLD = 2
H_VECTOR = 3
RUN = 8

FLOPS = 2 * (SL + 1) * BS * DM * DP


def every_second(row_words, g, u):
    first = g * HALVES * P + u
    return row_words[:, first : (g + 1) * HALVES * P : HALVES]


def from_split(split_words, g, u):
    first = (u * PASSES + g) * P
    return split_words[:, first : first + P]


def transpose_rows(nc, banks, ident, row_words, pick):
    bank = banks.tile([P, CHUNKS, P], F32)
    for c in range(CHUNKS):
        g, u = divmod(c, HALVES)
        nc.tensor.transpose(bank[:, c, :], pick(row_words, g, u), ident[:])
    return bank


def by_pass_row_half(bank):
    return bank[:].rearrange("p (g u) r -> p g r u", u=HALVES)


def split_rows(nc, pool, rows, name):
    split = pool.tile([P, DM], BF16, name=name)
    nc.vector.tensor_copy(
        out=split[:].rearrange("p (u c e) -> p u c e", u=HALVES, e=2 * RUN),
        in_=rows.rearrange("p (c u e) -> p u c e", u=HALVES, e=2 * RUN),
    )
    return split


def tile_multiheadattention_pa_t_kernel(tc, query, keys, Wq, Wk, out):
    nc = tc.nc
    with ExitStack() as ctx:
        const = ctx.enter_context(tc.tile_pool(name="const", bufs=1))
        resident = ctx.enter_context(tc.tile_pool(name="resident", bufs=SL // S_LOAD))
        stage = ctx.enter_context(tc.tile_pool(name="stage", bufs=4))
        banks = ctx.enter_context(tc.psum_pool(name="banks", bufs=4))
        sums = ctx.enter_context(tc.psum_pool(name="sums", bufs=4))
        ctx.enter_context(tc.manual_schedule())

        key_rows = []

        def load_keys(first, last):
            for i in range(first, last):
                rows = resident.tile([P, S_LOAD * DM], BF16, name="rows")
                nc.sync.dma_start(
                    out=rows[:].rearrange("b (s k) -> b s k", s=S_LOAD),
                    in_=keys[i * S_LOAD : (i + 1) * S_LOAD].rearrange("s b k -> b s k"),
                )
                key_rows.append(rows)

        def load_weight(w, name):
            parts = []
            for r in range(DP // P):
                part = const.tile([P, DM], BF16, name=f"{name}_rows_{r}")
                nc.sync.dma_start(out=part[:], in_=w[r * P : (r + 1) * P])
                parts.append(part)
            return parts

        wk_rows = load_weight(Wk, "wk")
        load_keys(0, 1)
        q_rows = const.tile([P, DM], BF16)
        nc.sync.dma_start(out=q_rows[:], in_=query)
        wq_rows = load_weight(Wq, "wq")
        load_keys(1, SL // S_LOAD)

        ident = const.tile([P, P], F32)
        make_identity(nc, ident[:])
        dot = const.tile([P, H, SL], F32)
        shifted = const.tile([P, (H + 1) * SL], F32)
        nc.gpsimd.memset(shifted[:, H * SL :], 0.0)

        def group_weight(parts, pick, name):
            grouped = const.tile([P, PASSES * DP * PACK], BF16, align_bytes=64, name=name + "_grouped")
            words = grouped[:].bitcast(F32).rearrange(
                "p (g r c u) -> p g r c u", g=PASSES, r=DP // P, u=HALVES
            )
            for part, r, copy in zip(parts, range(DP // P), (nc.scalar.copy, nc.vector.tensor_copy)):
                bank = transpose_rows(nc, banks, ident, part[:].bitcast(F32), pick)
                copy(out=words[:, :, r, :, :], in_=by_pass_row_half(bank))
            return grouped

        def split_weight(parts, name):
            return [split_rows(nc, const, part[:], f"{name}_split_{r}") for r, part in enumerate(parts)]

        def quantise(grouped, columns, name):
            codes = const.tile([P, columns], U32, align_bytes=64, name=name + "_codes")
            scales = const.tile([P, columns], U8, align_bytes=64, name=name + "_scales")
            nc.vector.quantize_mx(out=codes[:].bitcast(FP8X4), scales=scales[:], in_=grouped[:])
            return codes, scales

        def project(acc, row_codes, row_scales, first_col, w_codes, w_scales):
            for g in range(PASSES):
                rows = slice(first_col + g * P, first_col + (g + 1) * P)
                chans = slice(g * DP, (g + 1) * DP)
                nc.tensor.matmul_mx(
                    out=acc,
                    lhsT=row_codes[:, rows].bitcast(FP8X4),
                    lhsT_scale=row_scales[:, rows],
                    rhs=w_codes[:, chans].bitcast(FP8X4),
                    rhs_scale=w_scales[:, chans],
                    start=(g == 0),
                    stop=(g == PASSES - 1),
                )

        def group_query(q_split):
            grouped = const.tile([P, DM], BF16, align_bytes=64, name="q_grouped")
            bank = transpose_rows(nc, banks, ident, q_split[:].bitcast(F32), from_split)
            nc.scalar.copy(
                out=grouped[:].bitcast(F32).rearrange("p (g r u) -> p g r u", g=PASSES, u=HALVES),
                in_=by_pass_row_half(bank),
            )
            return grouped

        def project_query(q_mx, wq_mx):
            acc = sums.tile([P, S_BANK * DP], F32, name="acc")
            project(acc[:, :DP], *q_mx, 0, *wq_mx)
            qp = const.tile([P, DP], F32)
            nc.scalar.mul(out=qp[:], in_=acc[:, :DP], mul=1.0 / math.sqrt(NH))
            return qp

        grouped_of = {}
        codes_of = {}
        acc_of = {}
        prod_of = {}
        folded_of = {}

        def live(i):
            return 0 <= i < ROUNDS

        def first_step(i):
            return sum(ROUND_STEPS[:i])

        def full(i):
            return ROUND_STEPS[i] == MAX_STEPS

        def step_rows(s):
            first = (s % S_LOAD) * DM
            return key_rows[s // S_LOAD][:, first : first + DM]

        def transpose_round(i):
            grouped = stage.tile([P, MAX_STEPS * DM], BF16, align_bytes=64, name="grouped")
            words = grouped[:].bitcast(F32)
            for j in range(ROUND_STEPS[i]):
                s = first_step(i) + j
                bank = transpose_rows(nc, banks, ident, step_rows(s).bitcast(F32), every_second)
                nc.scalar.copy(
                    out=words[:, j * WORDS : (j + 1) * WORDS].rearrange(
                        "p (g r u) -> p g r u", g=PASSES, u=HALVES
                    ),
                    in_=by_pass_row_half(bank),
                )
            grouped_of[i] = grouped

        def quantise_round(i):
            columns = ROUND_STEPS[i] * PASSES * P
            codes = stage.tile([P, MAX_STEPS * PASSES * P], U32, align_bytes=64, name="codes")
            scales = stage.tile([P, MAX_STEPS * PASSES * P], U8, align_bytes=64, name="scales")
            nc.vector.quantize_mx(
                out=codes[:, :columns].bitcast(FP8X4),
                scales=scales[:, :columns],
                in_=grouped_of[i][:, : columns * PACK],
            )
            codes_of[i] = (codes, scales)

        def project_round(i):
            codes, scales = codes_of[i]
            acc = sums.tile([P, S_BANK * DP], F32, name="acc")
            for j in range(ROUND_STEPS[i]):
                project(acc[:, j * DP : (j + 1) * DP], codes, scales, j * PASSES * P, *wk_mx)
            acc_of[i] = acc

        def multiply_round(i):
            steps = ROUND_STEPS[i]
            prod = stage.tile([P, MAX_STEPS * DP], F32, name="prod")
            nc.vector.tensor_tensor(
                out=prod[:, : steps * DP].rearrange("p (s c) -> p s c", s=steps),
                in0=acc_of[i][:, : steps * DP].rearrange("p (s c) -> p s c", s=steps),
                in1=qp[:].unsqueeze(1).to_broadcast([P, steps, DP]),
                op=ALU.mult,
            )
            prod_of[i] = prod

        def by_head(i):
            return prod_of[i][:].rearrange("p (s h j) -> p s h j", s=MAX_STEPS, h=H)

        def fold_round(i):
            if full(i):
                halves = prod_of[i][:].rearrange("p (s h t j) -> p s h t j", s=MAX_STEPS, h=H, t=2)
                folded = stage.tile([P, MAX_STEPS, H_FOLD, NH // 2], F32, name="folded")
                nc.gpsimd.tensor_tensor(
                    out=folded[:],
                    in0=halves[:, :, :H_FOLD, 0, :],
                    in1=halves[:, :, :H_FOLD, 1, :],
                    op=ALU.add,
                )
                folded_of[i] = folded
            unused = stage.tile([P, MAX_STEPS, H - H_VECTOR, NH], F32, name="unused")
            for j in range(ROUND_STEPS[i]):
                s = first_step(i) + j
                for h in range(H_VECTOR, H):
                    nc.scalar.activation(
                        out=unused[:, j, h - H_VECTOR, :],
                        in_=by_head(i)[:, j, h, :],
                        func=ACT.Copy,
                        accum_out=dot[:, h, s : s + 1],
                    )

        def add_up(i, heads, terms):
            nc.vector.tensor_reduce(
                out=dot[:, heads, first_step(i) : first_step(i) + ROUND_STEPS[i]],
                in_=terms.rearrange("p s h j -> p h s j"),
                axis=AXIS.X,
                op=ALU.add,
            )

        def sum_round(i):
            first_whole = H_FOLD if full(i) else 0
            if first_whole < H_VECTOR:
                add_up(
                    i,
                    slice(first_whole, H_VECTOR),
                    by_head(i)[:, : ROUND_STEPS[i], first_whole:H_VECTOR, :],
                )
            if full(i):
                add_up(i, slice(0, H_FOLD), folded_of[i][:])

        wk_grouped = group_weight(wk_rows, every_second, "wk")
        transpose_round(0)
        q_split = split_rows(nc, const, q_rows[:], "q_split")
        wq_split = split_weight(wq_rows, "wq")
        wk_mx = quantise(wk_grouped, PASSES * DP, "wk")
        q_grouped = group_query(q_split)
        wq_grouped = group_weight(wq_split, from_split, "wq")
        for step in range(1, ROUNDS + LAG_SUM):
            if live(step):
                transpose_round(step)
            if live(step - LAG_MULTIPLY):
                multiply_round(step - LAG_MULTIPLY)
            if live(step - LAG_PROJECT):
                quantise_round(step - LAG_PROJECT)
                project_round(step - LAG_PROJECT)
            if step == LAG_PROJECT:
                q_mx = quantise(q_grouped, PASSES * P, "q")
                wq_mx = quantise(wq_grouped, PASSES * DP, "wq")
                qp = project_query(q_mx, wq_mx)
            if live(step - LAG_MULTIPLY):
                fold_round(step - LAG_MULTIPLY)
            if live(step - LAG_SUM):
                sum_round(step - LAG_SUM)

        neg_max = const.tile([P, H], F32)
        nc.vector.tensor_reduce(out=neg_max[:], in_=dot[:], axis=AXIS.X, op=ALU.max, negate=True)
        expd = const.tile([P, H, SL], F32)
        exp_sum = const.tile([P, H], F32)
        for h in range(H):
            nc.scalar.activation(
                out=expd[:, h, :],
                in_=dot[:, h, :],
                func=ACT.Exp,
                bias=neg_max[:, h : h + 1],
                scale=1.0,
                accum_out=exp_sum[:, h : h + 1],
            )
        nc.vector.tensor_tensor(
            out=shifted[:, : H * SL].rearrange("p (h s) -> p h s", h=H),
            in0=dot[:],
            in1=neg_max[:].unsqueeze(2).to_broadcast([P, H, SL]),
            op=ALU.add,
        )

        flipped = banks.tile([P, H, P], F32, name="bank")
        for h in range(H):
            nc.tensor.transpose(flipped[:, h, :], shifted[:, h * SL : h * SL + P], ident[:])
        spread = banks.tile([P, H, P], F32, name="bank")
        for h in range(H):
            nc.tensor.transpose(spread[:, h, :], exp_sum[:, h : h + 1].to_broadcast([P, P]), ident[:])
        for first in range(0, BS, BS // 2):
            half = slice(first, first + BS // 2)
            log_sum = const.tile([P, BS // 2, H], F32, name=f"log_sum_{first}")
            nc.scalar.activation(
                out=log_sum[:SL], in_=spread[:SL, :, half].rearrange("s h b -> s b h"), func=ACT.Ln
            )
            rows_out = const.tile([P, BS // 2, H], F32, name=f"rows_out_{first}")
            nc.vector.tensor_tensor(
                out=rows_out[:SL],
                in0=flipped[:SL, :, half].rearrange("s h b -> s b h"),
                in1=log_sum[:SL],
                op=ALU.subtract,
            )
            nc.sync.dma_start(
                out=out[:, half, :].rearrange("s b h -> s (b h)"),
                in_=rows_out[:SL].rearrange("s b h -> s (b h)"),
            )
